import numpy as np
import ml_dtypes


def mxq(x, axis, fmt="e4m3"):
    dtype, down = {"e4m3": (ml_dtypes.float8_e4m3fn, 7), "e5m2": (ml_dtypes.float8_e5m2, 14)}[fmt]
    v = np.moveaxis(np.asarray(x, np.float32).astype(ml_dtypes.bfloat16).astype(np.float64), axis, -1)
    blocks = v.reshape(v.shape[:-1] + (-1, 32))
    amax = np.abs(blocks).max(-1, keepdims=True)
    byte = np.maximum(np.where(amax > 0, np.frexp(amax)[1] - 1 + 127, 0) - down, 1)
    scale = np.exp2(byte - 127.0)
    codes = (blocks / scale).astype(np.float32).astype(dtype).astype(np.float64)
    return np.moveaxis((codes * scale).reshape(v.shape), -1, axis)


WIDE = False


def mx_kscale(k):
    if not WIDE:
        return np.ones(k)
    levels = np.array([10, -10, 5, -5, 0])
    a = np.random.permutation(np.resize(levels, k // 512 * 4)).reshape(k // 512, 4)
    idx = np.arange(k)
    return np.exp2(a[idx // 512, idx % 128 // 32])


BF16 = ml_dtypes.bfloat16


def bf(x):
    return np.asarray(x, np.float32).astype(BF16)


def f64(x):
    return np.asarray(x).astype(np.float64)


E2M1 = np.array([0.0, 0.5, 1.0, 1.5, 2.0, 3.0, 4.0, 6.0, -0.0, -0.5, -1.0, -1.5, -2.0, -3.0, -4.0, -6.0])


def pack_weight(w, fmt):
    k, n = w.shape
    w = f64(bf(w)).reshape(k // 32, 32, n)
    amax = np.abs(w).max(1)
    if fmt == "e4m3":
        byte = np.frexp(amax)[1] - 1 + 127 - 7
    else:
        mant, ex = np.frexp(amax / 6.0)
        byte = np.where(mant > 0.5, ex, ex - 1) + 127
    byte = np.clip(np.where(amax > 0, byte, 1), 1, 254)
    scaled = (w * np.exp2(127.0 - byte)[:, None, :]).reshape(k, n).astype(np.float32)
    by_word = np.ascontiguousarray(scaled.reshape(k // 512, 128, 4, n).transpose(0, 1, 3, 2))
    if fmt == "e4m3":
        words = by_word.astype(ml_dtypes.float8_e4m3fn).view(np.uint8)
    else:
        c = by_word.astype(ml_dtypes.float4_e2m1fn).view(np.uint8) & 0xF
        words = c[..., 0::2] | (c[..., 1::2] << 4)
    return np.ascontiguousarray(words), np.ascontiguousarray(byte.astype(np.uint8).reshape(k // 512, 16, n))


def unpack_weight(words, scales, fmt):
    g, p, n, _ = words.shape
    if fmt == "e4m3":
        vals = np.ascontiguousarray(words).view(ml_dtypes.float8_e4m3fn).astype(np.float64)
    else:
        nib = np.empty((g, p, n, 4), np.uint8)
        nib[..., 0::2] = words & 0xF
        nib[..., 1::2] = words >> 4
        vals = E2M1[nib]
    vals = vals * np.repeat(np.exp2(scales.astype(np.float64) - 127.0), 8, axis=1)[..., None]
    return vals.transpose(0, 1, 3, 2).reshape(g * 512, n)

def pack4(w):
    words, scales = pack_weight(w, "e2m1")
    return words.reshape(words.shape[0], 128, -1), scales


def unpack4(words, scales):
    return unpack_weight(words.reshape(words.shape[0], 128, -1, 2), scales, "e2m1")


T, B, I, H = 16, 128, 512, 1024


def sigmoid(v):
    return 1.0 / (1.0 + np.exp(-v))


def setup_inputs():
    s = mx_kscale(I)
    input_seq = bf(np.random.standard_normal((T, B, I)) * s)
    w = np.random.standard_normal((3 * H, I)) / np.sqrt(I) / s[None, :]
    words, scales = pack4(np.ascontiguousarray(w.T))
    b_ih = bf(np.random.standard_normal(3 * H) * 0.3)
    gh = bf(np.random.standard_normal((B, 3 * H)) * 0.5)
    return {"input_seq": input_seq,
            "W_ih_words": words,
            "W_ih_scales": scales,
            "b_ih": b_ih,
            "gh": gh}


def reference(input_seq, W_ih_words, W_ih_scales, b_ih, gh):
    gi = (mxq(f64(input_seq), 2, "e4m3") @ unpack4(W_ih_words, W_ih_scales)) + f64(b_ih)
    g = f64(gh)
    i_r, i_z, i_n = gi[..., :H], gi[..., H:2 * H], gi[..., 2 * H:]
    h_r, h_z, h_n = g[..., :H], g[..., H:2 * H], g[..., 2 * H:]
    r = sigmoid(i_r + h_r)
    z = sigmoid(i_z + h_z)
    n = np.tanh(i_n + r * h_n)
    h = (1.0 - z) * n
    return np.transpose(h, (1, 0, 2))

@@ -1,0 +1,268 @@
+from contextlib import ExitStack
+
+import concourse.mybir as mybir
+from concourse.masks import make_identity
+
+F32 = mybir.dt.float32
+BF16 = mybir.dt.bfloat16
+I32 = mybir.dt.int32
+U32 = mybir.dt.uint32
+U8 = mybir.dt.uint8
+FP8X4 = mybir.dt.float8_e4m3fn_x4
+FP4X4 = mybir.dt.float4_e2m1fn_x4
+ADD = mybir.AluOpType.add
+MULT = mybir.AluOpType.mult
+ACT = mybir.ActivationFunctionType
+
+P = 128
+T_STEPS = 16
+K = 512
+H = 1024
+BANK = 512
+T_GROUP = BANK // P
+N_GROUPS = T_STEPS // T_GROUP
+PAIRS = T_GROUP // 2
+BLOCKS = H // P
+N_UNITS = N_GROUPS * BLOCKS
+WORDS = K // 2
+GATE_R, GATE_Z, GATE_N = 0, 1, 2
+Z_LAG = 2
+SUM_LAG = 2
+TANH_LAG = 3
+OUT_LAG = 4
+
+FLOPS = 2 * T_STEPS * P * K * 3 * H
+
+
+def tile_grucellmodel_pa_kernel(tc, input_seq, W_ih_words, W_ih_scales, b_ih, gh, out):
+    nc = tc.nc
+    with ExitStack() as ctx:
+        ctx.enter_context(tc.manual_schedule())
+        const = ctx.enter_context(tc.tile_pool(name="const", bufs=1))
+        work = ctx.enter_context(tc.tile_pool(name="work", bufs=2))
+        psum = ctx.enter_context(tc.psum_pool(name="psum", bufs=2))
+
+        warm = const.tile([P, 1], F32)
+        nc.vector.memset(warm[:], 0.0)
+        nc.scalar.activation(out=warm[:], in_=warm[:], func=ACT.Sigmoid)
+        b_rows = const.tile([P, P], BF16)
+        nc.vector.memset(b_rows[:], 0.0)
+        w_scales = const.tile([P, 3 * H], U8, align_bytes=64)
+        nc.vector.memset(w_scales[:].bitcast(I32), 0)
+        bz_row = const.tile([P, H], BF16)
+        nc.vector.memset(bz_row[:], 0.0)
+        ident_f32 = const.tile([P, P], F32)
+        make_identity(nc, ident_f32[:])
+        ident_bf16 = const.tile([P, P], BF16)
+        make_identity(nc, ident_bf16[:])
+        ones = const.tile([P, P], BF16)
+        nc.gpsimd.memset(ones[:], 1.0)
+
+        x_sb = []
+        for c in range(N_GROUPS):
+            x_sb.append(const.tile([P, T_GROUP, K], BF16, name="x_sb%d" % c))
+        w_words = const.tile([P, 2 * 3 * H], U8, align_bytes=64)
+        gh_sb = const.tile([P, 3 * H], BF16)
+
+        def load_x(c):
+            nc.sync.dma_start(
+                out=x_sb[c][:],
+                in_=input_seq[c * T_GROUP : (c + 1) * T_GROUP].rearrange("t b k -> b t k"),
+            )
+
+        def load_w(gate):
+            nc.sync.dma_start(
+                out=w_words[:, 2 * gate * H : 2 * (gate + 1) * H].bitcast(I32),
+                in_=W_ih_words[0, :, 2 * gate * H : 2 * (gate + 1) * H].bitcast(I32),
+            )
+
+        def load_gh(gate):
+            nc.sync.dma_start(out=gh_sb[:, gate * H : (gate + 1) * H], in_=gh[:, gate * H : (gate + 1) * H])
+
+        load_x(0)
+        nc.scalar.dma_start(out=b_rows[0 : 3 * BLOCKS, :], in_=b_ih.rearrange("(c p) -> c p", p=P))
+        for q in range(4):
+            nc.sync.dma_start(
+                out=w_scales[32 * q : 32 * q + 4, :].bitcast(I32),
+                in_=W_ih_scales[0, 4 * q : 4 * q + 4, :].bitcast(I32),
+            )
+        load_w(GATE_R)
+        load_gh(GATE_R)
+        load_gh(GATE_N)
+        load_w(GATE_Z)
+        load_w(GATE_N)
+        load_gh(GATE_Z)
+        nc.scalar.dma_start(
+            out=bz_row[0:1, :], in_=b_ih[GATE_Z * H : (GATE_Z + 1) * H].rearrange("(o n) -> o n", o=1)
+        )
+        for c in range(1, N_GROUPS):
+            load_x(c)
+
+        x_codes = const.tile([P, T_STEPS * P], U32, align_bytes=64)
+        x_scales = const.tile([P, T_STEPS * P], U8, align_bytes=64)
+        grouped = {}
+
+        def regroup_x(pair):
+            c, i = divmod(pair, PAIRS)
+            xt = psum.tile([P, 2, 2, P], F32, tag="t", name="xt")
+            for tt in range(2):
+                x_words = x_sb[c][:, 2 * i + tt, :].bitcast(F32)
+                for u in range(2):
+                    nc.tensor.transpose(xt[:, tt, u, :], x_words[:, u:WORDS:2], ident_f32[:])
+            grouped[pair] = work.tile([P, 2 * P * 4], BF16, align_bytes=64, name="grouped")
+            nc.scalar.copy(
+                out=grouped[pair][:].bitcast(F32).rearrange("p (t b u) -> p t b u", t=2, u=2),
+                in_=xt[:].rearrange("p t u b -> p t b u"),
+            )
+
+        def quantise_x(pair):
+            cols = slice(pair * 2 * P, (pair + 1) * 2 * P)
+            nc.vector.quantize_mx(
+                out=x_codes[:, cols].bitcast(FP8X4), scales=x_scales[:, cols], in_=grouped[pair][:]
+            )
+
+        def w_block(gate, jb):
+            first = gate * H + jb * P
+            return (w_words[:, 2 * first : 2 * (first + P)].bitcast(FP4X4), w_scales[:, first : first + P])
+
+        def x_block(first, width):
+            return (x_codes[:, first : first + width].bitcast(FP8X4), x_scales[:, first : first + width])
+
+        def over_time(block):
+            return block.unsqueeze(1).to_broadcast([P, T_GROUP, P])
+
+        def flat(tile3):
+            return tile3.rearrange("p t b -> p (t b)")
+
+        b_col = const.tile([P, 3 * BLOCKS], F32)
+        ghT_r = const.tile([P, BLOCKS, P], BF16)
+        ghT_n = const.tile([P, BLOCKS, P], BF16)
+        ghb_z = const.tile([P, H], F32)
+
+        def transpose_gh(gate):
+            gt = psum.tile([P, BLOCKS, P], BF16, tag="z", name="gt")
+            for jb in range(BLOCKS):
+                first = gate * H + jb * P
+                nc.tensor.transpose(gt[:, jb, :], gh_sb[:, first : first + P], ident_bf16[:])
+            return gt
+
+        def prepare_z():
+            for half in range(H // BANK):
+                cols = slice(half * BANK, (half + 1) * BANK)
+                bz = psum.tile([P, BANK], F32, tag="t", name="bz")
+                nc.tensor.matmul(bz[:], lhsT=ones[:], rhs=bz_row[:, cols], start=True, stop=True)
+                nc.vector.tensor_tensor(
+                    out=ghb_z[:, cols],
+                    in0=bz[:],
+                    in1=gh_sb[:, GATE_Z * H + half * BANK : GATE_Z * H + (half + 1) * BANK],
+                    op=ADD,
+                )
+
+        pr, pz, pn, st = {}, {}, {}, {}
+        m, zc, n_new = {}, {}, {}
+
+        def matmul_transposed(acc, gate, u):
+            c, jb = divmod(u, BLOCKS)
+            w, w_scale = w_block(gate, jb)
+            x, x_scale = x_block(c * BANK, BANK)
+            nc.tensor.matmul_mx(flat(acc[:]), lhsT=w, lhsT_scale=w_scale, rhs=x, rhs_scale=x_scale, start=True, stop=True)
+
+        def matmul_r(u):
+            pr[u] = psum.tile([P, T_GROUP, P], F32, tag="r", name="pr")
+            matmul_transposed(pr[u], GATE_R, u)
+
+        def matmul_n(u):
+            pn[u] = psum.tile([P, T_GROUP, P], F32, tag="n", name="pn")
+            matmul_transposed(pn[u], GATE_N, u)
+
+        def matmul_z(u):
+            c, jb = divmod(u, BLOCKS)
+            w, w_scale = w_block(GATE_Z, jb)
+            pz[u] = psum.tile([P, T_GROUP, P], F32, tag="z", name="pz")
+            for tt in range(T_GROUP):
+                x, x_scale = x_block((c * T_GROUP + tt) * P, P)
+                nc.tensor.matmul_mx(pz[u][:, tt, :], lhsT=x, lhsT_scale=x_scale, rhs=w, rhs_scale=w_scale, start=True, stop=True)
+
+        def reset_gate(u):
+            jb = u % BLOCKS
+            a_r = work.tile([P, T_GROUP, P], F32, name="a_r")
+            nc.vector.tensor_tensor(out=a_r[:], in0=pr[u][:], in1=over_time(ghT_r[:, jb, :]), op=ADD)
+            r = work.tile([P, T_GROUP, P], F32, name="r", bufs=3)
+            nc.scalar.activation(out=r[:], in_=a_r[:], func=ACT.Sigmoid, bias=b_col[:, jb : jb + 1])
+            m[u] = work.tile([P, T_GROUP, P], F32, name="m", bufs=4)
+            nc.gpsimd.tensor_tensor(out=m[u][:], in0=r[:], in1=over_time(ghT_n[:, jb, :]), op=MULT)
+
+        def update_gate(u):
+            jb = u % BLOCKS
+            a_z = work.tile([P, T_GROUP, P], F32, name="a_z")
+            nc.vector.tensor_tensor(out=a_z[:], in0=pz[u][:], in1=over_time(ghb_z[:, jb * P : (jb + 1) * P]), op=ADD)
+            zc[u] = work.tile([P, T_GROUP, P], F32, name="zc", bufs=4)
+            nc.scalar.activation(out=zc[u][:], in_=a_z[:], func=ACT.Sigmoid, scale=-1.0)
+
+        def candidate_sum(u):
+            jb = u % BLOCKS
+            s = work.tile([P, T_GROUP, P], F32, name="s")
+            nc.vector.scalar_tensor_tensor(
+                out=flat(s[:]),
+                in0=flat(pn[u][:]),
+                scalar=b_col[:, GATE_N * BLOCKS + jb : GATE_N * BLOCKS + jb + 1],
+                in1=flat(m[u][:]),
+                op0=ADD,
+                op1=ADD,
+            )
+            st[u] = psum.tile([P, T_GROUP, P], F32, tag="t", name="st")
+            for tt in range(T_GROUP):
+                nc.tensor.transpose(st[u][:, tt, :], s[:, tt, :], ident_f32[:])
+
+        def candidate_tanh(u):
+            n_new[u] = work.tile([P, T_GROUP, P], F32, name="n_new", bufs=3)
+            nc.scalar.activation(out=n_new[u][:], in_=st[u][:], func=ACT.Tanh)
+
+        def output(u):
+            c, jb = divmod(u, BLOCKS)
+            h = work.tile([P, T_GROUP, P], F32, name="h", bufs=4)
+            engine = nc.gpsimd if u % 2 == 0 else nc.vector
+            engine.tensor_tensor(out=h[:], in0=zc[u][:], in1=n_new[u][:], op=MULT)
+            nc.sync.dma_start(out=out[:, c * T_GROUP : (c + 1) * T_GROUP, jb * P : (jb + 1) * P], in_=h[:])
+
+        for pair in range(PAIRS):
+            regroup_x(pair)
+        for pair in range(PAIRS):
+            quantise_x(pair)
+        bt = psum.tile([P, P], BF16, tag="n")
+        nc.tensor.transpose(bt[:], b_rows[:], ident_bf16[:])
+        nc.vector.tensor_copy(out=b_col[:], in_=bt[:, 0 : 3 * BLOCKS])
+        nc.vector.tensor_copy(out=ghT_r[:], in_=transpose_gh(GATE_R)[:])
+        nc.scalar.copy(out=ghT_n[:], in_=transpose_gh(GATE_N)[:])
+        matmul_r(0)
+
+        def in_range(u):
+            return 0 <= u < N_UNITS
+
+        for step in range(N_UNITS + OUT_LAG):
+            c, jb = divmod(step, BLOCKS)
+            regroup_pair = jb - BLOCKS // 2
+            quantise_pair = regroup_pair - 1
+            next_group = c + 1 < N_GROUPS
+            if in_range(step + 1):
+                matmul_r(step + 1)
+            if in_range(step + 1 - Z_LAG):
+                matmul_z(step + 1 - Z_LAG)
+            if in_range(step + 1 - SUM_LAG):
+                matmul_n(step + 1 - SUM_LAG)
+            if in_range(step):
+                reset_gate(step)
+            if step == Z_LAG:
+                prepare_z()
+            if in_range(step - Z_LAG):
+                update_gate(step - Z_LAG)
+            if in_range(step - SUM_LAG):
+                candidate_sum(step - SUM_LAG)
+            if in_range(step - TANH_LAG):
+                candidate_tanh(step - TANH_LAG)
+            if next_group and 0 <= regroup_pair < PAIRS:
+                regroup_x((c + 1) * PAIRS + regroup_pair)
+            if in_range(step - OUT_LAG):
+                output(step - OUT_LAG)
+            if next_group and 0 <= quantise_pair < PAIRS:
+                quantise_x((c + 1) * PAIRS + quantise_pair)

@@ -221,8 +221,7 @@ def tile_grucellmodel_pa_kernel(tc, input_seq, W_ih_words, W_ih_scales, b_ih, gh
         def output(u):
             c, jb = divmod(u, BLOCKS)
             h = work.tile([P, T_GROUP, P], F32, name="h", bufs=4)
-            engine = nc.gpsimd if u % 2 == 0 else nc.vector
-            engine.tensor_tensor(out=h[:], in0=zc[u][:], in1=n_new[u][:], op=MULT)
+            nc.vector.tensor_tensor(out=h[:], in0=zc[u][:], in1=n_new[u][:], op=MULT)
             nc.sync.dma_start(out=out[:, c * T_GROUP : (c + 1) * T_GROUP, jb * P : (jb + 1) * P], in_=h[:])
 
         for pair in range(PAIRS):

@@ -28,8 +28,9 @@ WORDS = K // 2
 GATE_R, GATE_Z, GATE_N = 0, 1, 2
 Z_LAG = 2
 SUM_LAG = 2
-TANH_LAG = 3
-OUT_LAG = 4
+TRANSPOSE_LAG = 3
+TANH_LAG = 4
+OUT_LAG = 5
 
 FLOPS = 2 * T_STEPS * P * K * 3 * H
 
@@ -79,8 +80,11 @@ def tile_grucellmodel_pa_kernel(tc, input_seq, W_ih_words, W_ih_scales, b_ih, gh
         def load_gh(gate):
             nc.sync.dma_start(out=gh_sb[:, gate * H : (gate + 1) * H], in_=gh[:, gate * H : (gate + 1) * H])
 
-        load_x(0)
         nc.scalar.dma_start(out=b_rows[0 : 3 * BLOCKS, :], in_=b_ih.rearrange("(c p) -> c p", p=P))
+        load_x(0)
+        nc.scalar.dma_start(
+            out=bz_row[0:1, :], in_=b_ih[GATE_Z * H : (GATE_Z + 1) * H].rearrange("(o n) -> o n", o=1)
+        )
         for q in range(4):
             nc.sync.dma_start(
                 out=w_scales[32 * q : 32 * q + 4, :].bitcast(I32),
@@ -92,9 +96,6 @@ def tile_grucellmodel_pa_kernel(tc, input_seq, W_ih_words, W_ih_scales, b_ih, gh
         load_w(GATE_Z)
         load_w(GATE_N)
         load_gh(GATE_Z)
-        nc.scalar.dma_start(
-            out=bz_row[0:1, :], in_=b_ih[GATE_Z * H : (GATE_Z + 1) * H].rearrange("(o n) -> o n", o=1)
-        )
         for c in range(1, N_GROUPS):
             load_x(c)
 
@@ -146,20 +147,26 @@ def tile_grucellmodel_pa_kernel(tc, input_seq, W_ih_words, W_ih_scales, b_ih, gh
                 nc.tensor.transpose(gt[:, jb, :], gh_sb[:, first : first + P], ident_bf16[:])
             return gt
 
-        def prepare_z():
+        bz = {}
+
+        def spread_bz():
             for half in range(H // BANK):
-                cols = slice(half * BANK, (half + 1) * BANK)
-                bz = psum.tile([P, BANK], F32, tag="t", name="bz")
-                nc.tensor.matmul(bz[:], lhsT=ones[:], rhs=bz_row[:, cols], start=True, stop=True)
+                bz[half] = psum.tile([P, BANK], F32, tag="t", name="bz")
+                nc.tensor.matmul(
+                    bz[half][:], lhsT=ones[:], rhs=bz_row[:, half * BANK : (half + 1) * BANK], start=True, stop=True
+                )
+
+        def add_bz_to_gh():
+            for half in range(H // BANK):
                 nc.vector.tensor_tensor(
-                    out=ghb_z[:, cols],
-                    in0=bz[:],
+                    out=ghb_z[:, half * BANK : (half + 1) * BANK],
+                    in0=bz[half][:],
                     in1=gh_sb[:, GATE_Z * H + half * BANK : GATE_Z * H + (half + 1) * BANK],
                     op=ADD,
                 )
 
         pr, pz, pn, st = {}, {}, {}, {}
-        m, zc, n_new = {}, {}, {}
+        m, s, zc, n_new = {}, {}, {}, {}
 
         def matmul_transposed(acc, gate, u):
             c, jb = divmod(u, BLOCKS)
@@ -189,30 +196,43 @@ def tile_grucellmodel_pa_kernel(tc, input_seq, W_ih_words, W_ih_scales, b_ih, gh
             nc.vector.tensor_tensor(out=a_r[:], in0=pr[u][:], in1=over_time(ghT_r[:, jb, :]), op=ADD)
             r = work.tile([P, T_GROUP, P], F32, name="r", bufs=3)
             nc.scalar.activation(out=r[:], in_=a_r[:], func=ACT.Sigmoid, bias=b_col[:, jb : jb + 1])
-            m[u] = work.tile([P, T_GROUP, P], F32, name="m", bufs=4)
+            m[u] = work.tile([P, T_GROUP, P], F32, name="m", bufs=5)
             nc.gpsimd.tensor_tensor(out=m[u][:], in0=r[:], in1=over_time(ghT_n[:, jb, :]), op=MULT)
 
         def update_gate(u):
             jb = u % BLOCKS
             a_z = work.tile([P, T_GROUP, P], F32, name="a_z")
             nc.vector.tensor_tensor(out=a_z[:], in0=pz[u][:], in1=over_time(ghb_z[:, jb * P : (jb + 1) * P]), op=ADD)
-            zc[u] = work.tile([P, T_GROUP, P], F32, name="zc", bufs=4)
+            zc[u] = work.tile([P, T_GROUP, P], F32, name="zc", bufs=5)
             nc.scalar.activation(out=zc[u][:], in_=a_z[:], func=ACT.Sigmoid, scale=-1.0)
 
-        def candidate_sum(u):
-            jb = u % BLOCKS
-            s = work.tile([P, T_GROUP, P], F32, name="s")
+        def on_scalar(u):
+            return u % 2 == 1
+
+        def candidate_sum_on_vector(u):
+            bn = b_col[:, GATE_N * BLOCKS + u % BLOCKS : GATE_N * BLOCKS + u % BLOCKS + 1]
+            s[u] = work.tile([P, T_GROUP, P], F32, name="s", bufs=3)
             nc.vector.scalar_tensor_tensor(
-                out=flat(s[:]),
-                in0=flat(pn[u][:]),
-                scalar=b_col[:, GATE_N * BLOCKS + jb : GATE_N * BLOCKS + jb + 1],
-                in1=flat(m[u][:]),
-                op0=ADD,
-                op1=ADD,
+                out=flat(s[u][:]), in0=flat(pn[u][:]), scalar=bn, in1=flat(m[u][:]), op0=ADD, op1=ADD
             )
+
+        def candidate_bias_on_scalar(u):
+            bn = b_col[:, GATE_N * BLOCKS + u % BLOCKS : GATE_N * BLOCKS + u % BLOCKS + 1]
+            s[u] = work.tile([P, T_GROUP, P], F32, name="s", bufs=3)
+            nc.scalar.activation(out=s[u][:], in_=pn[u][:], func=ACT.Identity, bias=bn)
+
+        def candidate_transpose(u):
             st[u] = psum.tile([P, T_GROUP, P], F32, tag="t", name="st")
             for tt in range(T_GROUP):
-                nc.tensor.transpose(st[u][:, tt, :], s[:, tt, :], ident_f32[:])
+                if on_scalar(u):
+                    nc.tensor.matmul(
+                        st[u][:, tt, :], lhsT=s[u][:, tt, :], rhs=ident_f32[:], is_transpose=True, start=True, stop=False
+                    )
+                    nc.tensor.matmul(
+                        st[u][:, tt, :], lhsT=m[u][:, tt, :], rhs=ident_f32[:], is_transpose=True, start=False, stop=True
+                    )
+                else:
+                    nc.tensor.transpose(st[u][:, tt, :], s[u][:, tt, :], ident_f32[:])
 
         def candidate_tanh(u):
             n_new[u] = work.tile([P, T_GROUP, P], F32, name="n_new", bufs=3)
@@ -233,35 +253,36 @@ def tile_grucellmodel_pa_kernel(tc, input_seq, W_ih_words, W_ih_scales, b_ih, gh
         nc.vector.tensor_copy(out=b_col[:], in_=bt[:, 0 : 3 * BLOCKS])
         nc.vector.tensor_copy(out=ghT_r[:], in_=transpose_gh(GATE_R)[:])
         nc.scalar.copy(out=ghT_n[:], in_=transpose_gh(GATE_N)[:])
+        spread_bz()
         matmul_r(0)
 
         def in_range(u):
             return 0 <= u < N_UNITS
 
         for step in range(N_UNITS + OUT_LAG):
-            c, jb = divmod(step, BLOCKS)
-            regroup_pair = jb - BLOCKS // 2
-            quantise_pair = regroup_pair - 1
-            next_group = c + 1 < N_GROUPS
             if in_range(step + 1):
                 matmul_r(step + 1)
             if in_range(step + 1 - Z_LAG):
                 matmul_z(step + 1 - Z_LAG)
             if in_range(step + 1 - SUM_LAG):
                 matmul_n(step + 1 - SUM_LAG)
+            if in_range(step - SUM_LAG) and on_scalar(step - SUM_LAG):
+                candidate_bias_on_scalar(step - SUM_LAG)
             if in_range(step):
                 reset_gate(step)
             if step == Z_LAG:
-                prepare_z()
+                add_bz_to_gh()
             if in_range(step - Z_LAG):
                 update_gate(step - Z_LAG)
-            if in_range(step - SUM_LAG):
-                candidate_sum(step - SUM_LAG)
+            if in_range(step - SUM_LAG) and not on_scalar(step - SUM_LAG):
+                candidate_sum_on_vector(step - SUM_LAG)
+            if in_range(step - TRANSPOSE_LAG):
+                candidate_transpose(step - TRANSPOSE_LAG)
             if in_range(step - TANH_LAG):
                 candidate_tanh(step - TANH_LAG)
-            if next_group and 0 <= regroup_pair < PAIRS:
-                regroup_x((c + 1) * PAIRS + regroup_pair)
+            if PAIRS <= step < N_GROUPS * PAIRS:
+                regroup_x(step)
             if in_range(step - OUT_LAG):
                 output(step - OUT_LAG)
-            if next_group and 0 <= quantise_pair < PAIRS:
-                quantise_x((c + 1) * PAIRS + quantise_pair)
+            if PAIRS <= step - 1 < N_GROUPS * PAIRS:
+                quantise_x(step - 1)

@@ -38,7 +38,6 @@ FLOPS = 2 * T_STEPS * P * K * 3 * H
 def tile_grucellmodel_pa_kernel(tc, input_seq, W_ih_words, W_ih_scales, b_ih, gh, out):
     nc = tc.nc
     with ExitStack() as ctx:
-        ctx.enter_context(tc.manual_schedule())
         const = ctx.enter_context(tc.tile_pool(name="const", bufs=1))
         work = ctx.enter_context(tc.tile_pool(name="work", bufs=2))
         psum = ctx.enter_context(tc.psum_pool(name="psum", bufs=2))

@@ -31,6 +31,8 @@ SUM_LAG = 2
 TRANSPOSE_LAG = 3
 TANH_LAG = 4
 OUT_LAG = 5
+Z_BUFS = 1
+N_BUFS = 2
 
 FLOPS = 2 * T_STEPS * P * K * 3 * H
 
@@ -136,11 +138,10 @@ def tile_grucellmodel_pa_kernel(tc, input_seq, W_ih_words, W_ih_scales, b_ih, gh
 
         b_col = const.tile([P, 3 * BLOCKS], F32)
         ghT_r = const.tile([P, BLOCKS, P], BF16)
-        ghT_n = const.tile([P, BLOCKS, P], BF16)
+        ghT_n = psum.tile([P, BLOCKS, P], BF16, tag="g", name="ghT_n", bufs=1)
         ghb_z = const.tile([P, H], F32)
 
-        def transpose_gh(gate):
-            gt = psum.tile([P, BLOCKS, P], BF16, tag="z", name="gt")
+        def transpose_gh(gate, gt):
             for jb in range(BLOCKS):
                 first = gate * H + jb * P
                 nc.tensor.transpose(gt[:, jb, :], gh_sb[:, first : first + P], ident_bf16[:])
@@ -178,13 +179,13 @@ def tile_grucellmodel_pa_kernel(tc, input_seq, W_ih_words, W_ih_scales, b_ih, gh
             matmul_transposed(pr[u], GATE_R, u)
 
         def matmul_n(u):
-            pn[u] = psum.tile([P, T_GROUP, P], F32, tag="n", name="pn")
+            pn[u] = psum.tile([P, T_GROUP, P], F32, tag="n", name="pn", bufs=N_BUFS)
             matmul_transposed(pn[u], GATE_N, u)
 
         def matmul_z(u):
             c, jb = divmod(u, BLOCKS)
             w, w_scale = w_block(GATE_Z, jb)
-            pz[u] = psum.tile([P, T_GROUP, P], F32, tag="z", name="pz")
+            pz[u] = psum.tile([P, T_GROUP, P], F32, tag="z", name="pz", bufs=Z_BUFS)
             for tt in range(T_GROUP):
                 x, x_scale = x_block((c * T_GROUP + tt) * P, P)
                 nc.tensor.matmul_mx(pz[u][:, tt, :], lhsT=x, lhsT_scale=x_scale, rhs=w, rhs_scale=w_scale, start=True, stop=True)
@@ -196,7 +197,7 @@ def tile_grucellmodel_pa_kernel(tc, input_seq, W_ih_words, W_ih_scales, b_ih, gh
             r = work.tile([P, T_GROUP, P], F32, name="r", bufs=3)
             nc.scalar.activation(out=r[:], in_=a_r[:], func=ACT.Sigmoid, bias=b_col[:, jb : jb + 1])
             m[u] = work.tile([P, T_GROUP, P], F32, name="m", bufs=5)
-            nc.gpsimd.tensor_tensor(out=m[u][:], in0=r[:], in1=over_time(ghT_n[:, jb, :]), op=MULT)
+            nc.vector.tensor_tensor(out=m[u][:], in0=r[:], in1=over_time(ghT_n[:, jb, :]), op=MULT)
 
         def update_gate(u):
             jb = u % BLOCKS
@@ -240,18 +241,19 @@ def tile_grucellmodel_pa_kernel(tc, input_seq, W_ih_words, W_ih_scales, b_ih, gh
         def output(u):
             c, jb = divmod(u, BLOCKS)
             h = work.tile([P, T_GROUP, P], F32, name="h", bufs=4)
-            nc.vector.tensor_tensor(out=h[:], in0=zc[u][:], in1=n_new[u][:], op=MULT)
+            nc.gpsimd.tensor_tensor(out=h[:], in0=zc[u][:], in1=n_new[u][:], op=MULT)
             nc.sync.dma_start(out=out[:, c * T_GROUP : (c + 1) * T_GROUP, jb * P : (jb + 1) * P], in_=h[:])
 
         for pair in range(PAIRS):
             regroup_x(pair)
         for pair in range(PAIRS):
             quantise_x(pair)
-        bt = psum.tile([P, P], BF16, tag="n")
+        bt = psum.tile([P, P], BF16, tag="n", name="bt", bufs=N_BUFS)
         nc.tensor.transpose(bt[:], b_rows[:], ident_bf16[:])
         nc.vector.tensor_copy(out=b_col[:], in_=bt[:, 0 : 3 * BLOCKS])
-        nc.vector.tensor_copy(out=ghT_r[:], in_=transpose_gh(GATE_R)[:])
-        nc.scalar.copy(out=ghT_n[:], in_=transpose_gh(GATE_N)[:])
+        gt_r = psum.tile([P, BLOCKS, P], BF16, tag="z", name="gt_r", bufs=Z_BUFS)
+        nc.vector.tensor_copy(out=ghT_r[:], in_=transpose_gh(GATE_R, gt_r)[:])
+        transpose_gh(GATE_N, ghT_n)
         spread_bz()
         matmul_r(0)
 

@@ -33,6 +33,8 @@ TANH_LAG = 4
 OUT_LAG = 5
 Z_BUFS = 1
 N_BUFS = 2
+SCALAR_FREE_UNITS = 6
+VECTOR_OUT_UNITS = 2
 
 FLOPS = 2 * T_STEPS * P * K * 3 * H
 
@@ -207,7 +209,7 @@ def tile_grucellmodel_pa_kernel(tc, input_seq, W_ih_words, W_ih_scales, b_ih, gh
             nc.scalar.activation(out=zc[u][:], in_=a_z[:], func=ACT.Sigmoid, scale=-1.0)
 
         def on_scalar(u):
-            return u % 2 == 1
+            return u % 2 == 1 and u < N_UNITS - SCALAR_FREE_UNITS
 
         def candidate_sum_on_vector(u):
             bn = b_col[:, GATE_N * BLOCKS + u % BLOCKS : GATE_N * BLOCKS + u % BLOCKS + 1]
@@ -241,7 +243,8 @@ def tile_grucellmodel_pa_kernel(tc, input_seq, W_ih_words, W_ih_scales, b_ih, gh
         def output(u):
             c, jb = divmod(u, BLOCKS)
             h = work.tile([P, T_GROUP, P], F32, name="h", bufs=4)
-            nc.gpsimd.tensor_tensor(out=h[:], in0=zc[u][:], in1=n_new[u][:], op=MULT)
+            engine = nc.vector if u >= N_UNITS - VECTOR_OUT_UNITS else nc.gpsimd
+            engine.tensor_tensor(out=h[:], in0=zc[u][:], in1=n_new[u][:], op=MULT)
             nc.sync.dma_start(out=out[:, c * T_GROUP : (c + 1) * T_GROUP, jb * P : (jb + 1) * P], in_=h[:])
 
         for pair in range(PAIRS):

@@ -141,6 +141,7 @@ def tile_grucellmodel_pa_kernel(tc, input_seq, W_ih_words, W_ih_scales, b_ih, gh
         b_col = const.tile([P, 3 * BLOCKS], F32)
         ghT_r = const.tile([P, BLOCKS, P], BF16)
         ghT_n = psum.tile([P, BLOCKS, P], BF16, tag="g", name="ghT_n", bufs=1)
+        ghT_n_sb = const.tile([P, BLOCKS, P], BF16)
         ghb_z = const.tile([P, H], F32)
 
         def transpose_gh(gate, gt):
@@ -192,6 +193,9 @@ def tile_grucellmodel_pa_kernel(tc, input_seq, W_ih_words, W_ih_scales, b_ih, gh
                 x, x_scale = x_block((c * T_GROUP + tt) * P, P)
                 nc.tensor.matmul_mx(pz[u][:, tt, :], lhsT=x, lhsT_scale=x_scale, rhs=w, rhs_scale=w_scale, start=True, stop=True)
 
+        def m_on_gpsimd(u):
+            return u % 4 == 1 and on_scalar(u)
+
         def reset_gate(u):
             jb = u % BLOCKS
             a_r = work.tile([P, T_GROUP, P], F32, name="a_r")
@@ -199,7 +203,10 @@ def tile_grucellmodel_pa_kernel(tc, input_seq, W_ih_words, W_ih_scales, b_ih, gh
             r = work.tile([P, T_GROUP, P], F32, name="r", bufs=3)
             nc.scalar.activation(out=r[:], in_=a_r[:], func=ACT.Sigmoid, bias=b_col[:, jb : jb + 1])
             m[u] = work.tile([P, T_GROUP, P], F32, name="m", bufs=5)
-            nc.vector.tensor_tensor(out=m[u][:], in0=r[:], in1=over_time(ghT_n[:, jb, :]), op=MULT)
+            if m_on_gpsimd(u):
+                nc.gpsimd.tensor_tensor(out=m[u][:], in0=r[:], in1=over_time(ghT_n_sb[:, jb, :]), op=MULT)
+            else:
+                nc.vector.tensor_tensor(out=m[u][:], in0=r[:], in1=over_time(ghT_n[:, jb, :]), op=MULT)
 
         def update_gate(u):
             jb = u % BLOCKS
@@ -257,6 +264,7 @@ def tile_grucellmodel_pa_kernel(tc, input_seq, W_ih_words, W_ih_scales, b_ih, gh
         gt_r = psum.tile([P, BLOCKS, P], BF16, tag="z", name="gt_r", bufs=Z_BUFS)
         nc.vector.tensor_copy(out=ghT_r[:], in_=transpose_gh(GATE_R, gt_r)[:])
         transpose_gh(GATE_N, ghT_n)
+        nc.scalar.copy(out=ghT_n_sb[:], in_=ghT_n[:])
         spread_bz()
         matmul_r(0)
 

@@ -31,8 +31,7 @@ SUM_LAG = 2
 TRANSPOSE_LAG = 3
 TANH_LAG = 4
 OUT_LAG = 5
-Z_BUFS = 1
-N_BUFS = 2
+MX_BUFS = 5
 SCALAR_FREE_UNITS = 6
 VECTOR_OUT_UNITS = 2
 
@@ -178,23 +177,23 @@ def tile_grucellmodel_pa_kernel(tc, input_seq, W_ih_words, W_ih_scales, b_ih, gh
             nc.tensor.matmul_mx(flat(acc[:]), lhsT=w, lhsT_scale=w_scale, rhs=x, rhs_scale=x_scale, start=True, stop=True)
 
         def matmul_r(u):
-            pr[u] = psum.tile([P, T_GROUP, P], F32, tag="r", name="pr")
+            pr[u] = psum.tile([P, T_GROUP, P], F32, tag="mx", name="pr", bufs=MX_BUFS)
             matmul_transposed(pr[u], GATE_R, u)
 
         def matmul_n(u):
-            pn[u] = psum.tile([P, T_GROUP, P], F32, tag="n", name="pn", bufs=N_BUFS)
+            pn[u] = psum.tile([P, T_GROUP, P], F32, tag="mx", name="pn", bufs=MX_BUFS)
             matmul_transposed(pn[u], GATE_N, u)
 
         def matmul_z(u):
             c, jb = divmod(u, BLOCKS)
             w, w_scale = w_block(GATE_Z, jb)
-            pz[u] = psum.tile([P, T_GROUP, P], F32, tag="z", name="pz", bufs=Z_BUFS)
+            pz[u] = psum.tile([P, T_GROUP, P], F32, tag="mx", name="pz", bufs=MX_BUFS)
             for tt in range(T_GROUP):
                 x, x_scale = x_block((c * T_GROUP + tt) * P, P)
                 nc.tensor.matmul_mx(pz[u][:, tt, :], lhsT=x, lhsT_scale=x_scale, rhs=w, rhs_scale=w_scale, start=True, stop=True)
 
         def m_on_gpsimd(u):
-            return u % 4 == 1 and on_scalar(u)
+            return on_scalar(u)
 
         def reset_gate(u):
             jb = u % BLOCKS
@@ -258,10 +257,10 @@ def tile_grucellmodel_pa_kernel(tc, input_seq, W_ih_words, W_ih_scales, b_ih, gh
             regroup_x(pair)
         for pair in range(PAIRS):
             quantise_x(pair)
-        bt = psum.tile([P, P], BF16, tag="n", name="bt", bufs=N_BUFS)
+        bt = psum.tile([P, P], BF16, tag="mx", name="bt", bufs=MX_BUFS)
         nc.tensor.transpose(bt[:], b_rows[:], ident_bf16[:])
         nc.vector.tensor_copy(out=b_col[:], in_=bt[:, 0 : 3 * BLOCKS])
-        gt_r = psum.tile([P, BLOCKS, P], BF16, tag="z", name="gt_r", bufs=Z_BUFS)
+        gt_r = psum.tile([P, BLOCKS, P], BF16, tag="mx", name="gt_r", bufs=MX_BUFS)
         nc.vector.tensor_copy(out=ghT_r[:], in_=transpose_gh(GATE_R, gt_r)[:])
         transpose_gh(GATE_N, ghT_n)
         nc.scalar.copy(out=ghT_n_sb[:], in_=ghT_n[:])

@@ -34,6 +34,7 @@ OUT_LAG = 5
 MX_BUFS = 5
 SCALAR_FREE_UNITS = 6
 VECTOR_OUT_UNITS = 2
+WARM_UP_MATMULS = 6
 
 FLOPS = 2 * T_STEPS * P * K * 3 * H
 
@@ -45,6 +46,11 @@ def tile_grucellmodel_pa_kernel(tc, input_seq, W_ih_words, W_ih_scales, b_ih, gh
         work = ctx.enter_context(tc.tile_pool(name="work", bufs=2))
         psum = ctx.enter_context(tc.psum_pool(name="psum", bufs=2))
 
+        zeros = const.tile([P, BANK], BF16)
+        nc.vector.memset(zeros[:], 0.0)
+        for i in range(WARM_UP_MATMULS):
+            idle = psum.tile([P, BANK], F32, tag="mx", name="idle", bufs=MX_BUFS)
+            nc.tensor.matmul(idle[:], lhsT=zeros[:, 0:P], rhs=zeros[:], start=True, stop=True)
         warm = const.tile([P, 1], F32)
         nc.vector.memset(warm[:], 0.0)
         nc.scalar.activation(out=warm[:], in_=warm[:], func=ACT.Sigmoid)
@@ -62,16 +68,13 @@ def tile_grucellmodel_pa_kernel(tc, input_seq, W_ih_words, W_ih_scales, b_ih, gh
         nc.gpsimd.memset(ones[:], 1.0)
 
         x_sb = []
-        for c in range(N_GROUPS):
-            x_sb.append(const.tile([P, T_GROUP, K], BF16, name="x_sb%d" % c))
+        for pair in range(N_GROUPS * PAIRS):
+            x_sb.append(const.tile([P, 2, K], BF16, name="x_sb%d" % pair))
         w_words = const.tile([P, 2 * 3 * H], U8, align_bytes=64)
         gh_sb = const.tile([P, 3 * H], BF16)
 
-        def load_x(c):
-            nc.sync.dma_start(
-                out=x_sb[c][:],
-                in_=input_seq[c * T_GROUP : (c + 1) * T_GROUP].rearrange("t b k -> b t k"),
-            )
+        def load_x(pair):
+            nc.sync.dma_start(out=x_sb[pair][:], in_=input_seq[2 * pair : 2 * pair + 2].rearrange("t b k -> b t k"))
 
         def load_w(gate):
             nc.sync.dma_start(
@@ -83,7 +86,8 @@ def tile_grucellmodel_pa_kernel(tc, input_seq, W_ih_words, W_ih_scales, b_ih, gh
             nc.sync.dma_start(out=gh_sb[:, gate * H : (gate + 1) * H], in_=gh[:, gate * H : (gate + 1) * H])
 
         nc.scalar.dma_start(out=b_rows[0 : 3 * BLOCKS, :], in_=b_ih.rearrange("(c p) -> c p", p=P))
-        load_x(0)
+        for pair in range(PAIRS):
+            load_x(pair)
         nc.scalar.dma_start(
             out=bz_row[0:1, :], in_=b_ih[GATE_Z * H : (GATE_Z + 1) * H].rearrange("(o n) -> o n", o=1)
         )
@@ -98,18 +102,17 @@ def tile_grucellmodel_pa_kernel(tc, input_seq, W_ih_words, W_ih_scales, b_ih, gh
         load_w(GATE_Z)
         load_w(GATE_N)
         load_gh(GATE_Z)
-        for c in range(1, N_GROUPS):
-            load_x(c)
+        for pair in range(PAIRS, N_GROUPS * PAIRS):
+            load_x(pair)
 
         x_codes = const.tile([P, T_STEPS * P], U32, align_bytes=64)
         x_scales = const.tile([P, T_STEPS * P], U8, align_bytes=64)
         grouped = {}
 
         def regroup_x(pair):
-            c, i = divmod(pair, PAIRS)
             xt = psum.tile([P, 2, 2, P], F32, tag="t", name="xt")
             for tt in range(2):
-                x_words = x_sb[c][:, 2 * i + tt, :].bitcast(F32)
+                x_words = x_sb[pair][:, tt, :].bitcast(F32)
                 for u in range(2):
                     nc.tensor.transpose(xt[:, tt, u, :], x_words[:, u:WORDS:2], ident_f32[:])
             grouped[pair] = work.tile([P, 2 * P * 4], BF16, align_bytes=64, name="grouped")
@@ -253,19 +256,19 @@ def tile_grucellmodel_pa_kernel(tc, input_seq, W_ih_words, W_ih_scales, b_ih, gh
             engine.tensor_tensor(out=h[:], in0=zc[u][:], in1=n_new[u][:], op=MULT)
             nc.sync.dma_start(out=out[:, c * T_GROUP : (c + 1) * T_GROUP, jb * P : (jb + 1) * P], in_=h[:])
 
+        bt = psum.tile([P, P], BF16, tag="mx", name="bt", bufs=MX_BUFS)
+        nc.tensor.transpose(bt[:], b_rows[:], ident_bf16[:])
+        nc.vector.tensor_copy(out=b_col[:], in_=bt[:, 0 : 3 * BLOCKS])
         for pair in range(PAIRS):
             regroup_x(pair)
         for pair in range(PAIRS):
             quantise_x(pair)
-        bt = psum.tile([P, P], BF16, tag="mx", name="bt", bufs=MX_BUFS)
-        nc.tensor.transpose(bt[:], b_rows[:], ident_bf16[:])
-        nc.vector.tensor_copy(out=b_col[:], in_=bt[:, 0 : 3 * BLOCKS])
         gt_r = psum.tile([P, BLOCKS, P], BF16, tag="mx", name="gt_r", bufs=MX_BUFS)
-        nc.vector.tensor_copy(out=ghT_r[:], in_=transpose_gh(GATE_R, gt_r)[:])
+        nc.scalar.copy(out=ghT_r[:], in_=transpose_gh(GATE_R, gt_r)[:])
+        matmul_r(0)
         transpose_gh(GATE_N, ghT_n)
         nc.scalar.copy(out=ghT_n_sb[:], in_=ghT_n[:])
         spread_bz()
-        matmul_r(0)
 
         def in_range(u):
             return 0 <= u < N_UNITS

@@ -34,7 +34,9 @@ OUT_LAG = 5
 MX_BUFS = 5
 SCALAR_FREE_UNITS = 6
 VECTOR_OUT_UNITS = 2
-WARM_UP_MATMULS = 6
+WARM_UP_MATMULS = 4
+EARLY_UNITS = 6
+FIRST_BLOCKS = 2
 
 FLOPS = 2 * T_STEPS * P * K * 3 * H
 
@@ -46,26 +48,24 @@ def tile_grucellmodel_pa_kernel(tc, input_seq, W_ih_words, W_ih_scales, b_ih, gh
         work = ctx.enter_context(tc.tile_pool(name="work", bufs=2))
         psum = ctx.enter_context(tc.psum_pool(name="psum", bufs=2))
 
-        zeros = const.tile([P, BANK], BF16)
+        zeros = const.tile([P, P], BF16)
         nc.vector.memset(zeros[:], 0.0)
-        for i in range(WARM_UP_MATMULS):
-            idle = psum.tile([P, BANK], F32, tag="mx", name="idle", bufs=MX_BUFS)
-            nc.tensor.matmul(idle[:], lhsT=zeros[:, 0:P], rhs=zeros[:], start=True, stop=True)
         warm = const.tile([P, 1], F32)
         nc.vector.memset(warm[:], 0.0)
         nc.scalar.activation(out=warm[:], in_=warm[:], func=ACT.Sigmoid)
-        b_rows = const.tile([P, P], BF16)
-        nc.vector.memset(b_rows[:], 0.0)
-        w_scales = const.tile([P, 3 * H], U8, align_bytes=64)
-        nc.vector.memset(w_scales[:].bitcast(I32), 0)
-        bz_row = const.tile([P, H], BF16)
-        nc.vector.memset(bz_row[:], 0.0)
         ident_f32 = const.tile([P, P], F32)
         make_identity(nc, ident_f32[:])
         ident_bf16 = const.tile([P, P], BF16)
         make_identity(nc, ident_bf16[:])
-        ones = const.tile([P, P], BF16)
-        nc.gpsimd.memset(ones[:], 1.0)
+        for i in range(WARM_UP_MATMULS):
+            idle = psum.tile([P, BANK], F32, tag="mx", name="idle", bufs=MX_BUFS)
+            nc.tensor.matmul(
+                idle[:], lhsT=zeros[:], rhs=zeros[:].unsqueeze(1).to_broadcast([P, T_GROUP, P]), start=True, stop=True
+            )
+        b_rows = const.tile([P, P], BF16)
+        nc.vector.memset(b_rows[:], 0.0)
+        w_scales = const.tile([P, 3 * H], U8, align_bytes=64)
+        nc.vector.memset(w_scales[:].bitcast(I32), 0)
 
         x_sb = []
         for pair in range(N_GROUPS * PAIRS):
@@ -85,23 +85,20 @@ def tile_grucellmodel_pa_kernel(tc, input_seq, W_ih_words, W_ih_scales, b_ih, gh
         def load_gh(gate):
             nc.sync.dma_start(out=gh_sb[:, gate * H : (gate + 1) * H], in_=gh[:, gate * H : (gate + 1) * H])
 
-        nc.scalar.dma_start(out=b_rows[0 : 3 * BLOCKS, :], in_=b_ih.rearrange("(c p) -> c p", p=P))
         for pair in range(PAIRS):
             load_x(pair)
-        nc.scalar.dma_start(
-            out=bz_row[0:1, :], in_=b_ih[GATE_Z * H : (GATE_Z + 1) * H].rearrange("(o n) -> o n", o=1)
-        )
+        nc.sync.dma_start(out=b_rows[0 : 3 * BLOCKS, :], in_=b_ih.rearrange("(c p) -> c p", p=P))
+        load_w(GATE_R)
+        load_gh(GATE_R)
         for q in range(4):
             nc.sync.dma_start(
                 out=w_scales[32 * q : 32 * q + 4, :].bitcast(I32),
                 in_=W_ih_scales[0, 4 * q : 4 * q + 4, :].bitcast(I32),
             )
-        load_w(GATE_R)
-        load_gh(GATE_R)
+        load_gh(GATE_Z)
         load_gh(GATE_N)
         load_w(GATE_Z)
         load_w(GATE_N)
-        load_gh(GATE_Z)
         for pair in range(PAIRS, N_GROUPS * PAIRS):
             load_x(pair)
 
@@ -116,7 +113,8 @@ def tile_grucellmodel_pa_kernel(tc, input_seq, W_ih_words, W_ih_scales, b_ih, gh
                 for u in range(2):
                     nc.tensor.transpose(xt[:, tt, u, :], x_words[:, u:WORDS:2], ident_f32[:])
             grouped[pair] = work.tile([P, 2 * P * 4], BF16, align_bytes=64, name="grouped")
-            nc.scalar.copy(
+            copy = nc.vector.tensor_copy if pair == 1 else nc.scalar.copy
+            copy(
                 out=grouped[pair][:].bitcast(F32).rearrange("p (t b u) -> p t b u", t=2, u=2),
                 in_=xt[:].rearrange("p t u b -> p t b u"),
             )
@@ -146,8 +144,8 @@ def tile_grucellmodel_pa_kernel(tc, input_seq, W_ih_words, W_ih_scales, b_ih, gh
         ghT_n_sb = const.tile([P, BLOCKS, P], BF16)
         ghb_z = const.tile([P, H], F32)
 
-        def transpose_gh(gate, gt):
-            for jb in range(BLOCKS):
+        def transpose_gh(gate, gt, first_block=0, last_block=BLOCKS):
+            for jb in range(first_block, last_block):
                 first = gate * H + jb * P
                 nc.tensor.transpose(gt[:, jb, :], gh_sb[:, first : first + P], ident_bf16[:])
             return gt
@@ -157,9 +155,15 @@ def tile_grucellmodel_pa_kernel(tc, input_seq, W_ih_words, W_ih_scales, b_ih, gh
         def spread_bz():
             for half in range(H // BANK):
                 bz[half] = psum.tile([P, BANK], F32, tag="t", name="bz")
-                nc.tensor.matmul(
-                    bz[half][:], lhsT=ones[:], rhs=bz_row[:, half * BANK : (half + 1) * BANK], start=True, stop=True
-                )
+                for i in range(BANK // P):
+                    c = GATE_Z * BLOCKS + half * (BANK // P) + i
+                    nc.tensor.matmul(
+                        bz[half][:, i * P : (i + 1) * P],
+                        lhsT=ident_bf16[:, c : c + 1].to_broadcast([P, P]),
+                        rhs=b_rows[:],
+                        start=True,
+                        stop=True,
+                    )
 
         def add_bz_to_gh():
             for half in range(H // BANK):
@@ -171,7 +175,7 @@ def tile_grucellmodel_pa_kernel(tc, input_seq, W_ih_words, W_ih_scales, b_ih, gh
                 )
 
         pr, pz, pn, st = {}, {}, {}, {}
-        m, s, zc, n_new = {}, {}, {}, {}
+        r, m, s, zc, n_new = {}, {}, {}, {}, {}
 
         def matmul_transposed(acc, gate, u):
             c, jb = divmod(u, BLOCKS)
@@ -196,19 +200,22 @@ def tile_grucellmodel_pa_kernel(tc, input_seq, W_ih_words, W_ih_scales, b_ih, gh
                 nc.tensor.matmul_mx(pz[u][:, tt, :], lhsT=x, lhsT_scale=x_scale, rhs=w, rhs_scale=w_scale, start=True, stop=True)
 
         def m_on_gpsimd(u):
-            return on_scalar(u)
+            return on_scalar(u) or u < EARLY_UNITS
 
         def reset_gate(u):
             jb = u % BLOCKS
             a_r = work.tile([P, T_GROUP, P], F32, name="a_r")
             nc.vector.tensor_tensor(out=a_r[:], in0=pr[u][:], in1=over_time(ghT_r[:, jb, :]), op=ADD)
-            r = work.tile([P, T_GROUP, P], F32, name="r", bufs=3)
-            nc.scalar.activation(out=r[:], in_=a_r[:], func=ACT.Sigmoid, bias=b_col[:, jb : jb + 1])
+            r[u] = work.tile([P, T_GROUP, P], F32, name="r", bufs=3)
+            nc.scalar.activation(out=r[u][:], in_=a_r[:], func=ACT.Sigmoid, bias=b_col[:, jb : jb + 1])
+
+        def reset_product(u):
+            jb = u % BLOCKS
             m[u] = work.tile([P, T_GROUP, P], F32, name="m", bufs=5)
             if m_on_gpsimd(u):
-                nc.gpsimd.tensor_tensor(out=m[u][:], in0=r[:], in1=over_time(ghT_n_sb[:, jb, :]), op=MULT)
+                nc.gpsimd.tensor_tensor(out=m[u][:], in0=r[u][:], in1=over_time(ghT_n_sb[:, jb, :]), op=MULT)
             else:
-                nc.vector.tensor_tensor(out=m[u][:], in0=r[:], in1=over_time(ghT_n[:, jb, :]), op=MULT)
+                nc.vector.tensor_tensor(out=m[u][:], in0=r[u][:], in1=over_time(ghT_n[:, jb, :]), op=MULT)
 
         def update_gate(u):
             jb = u % BLOCKS
@@ -218,7 +225,7 @@ def tile_grucellmodel_pa_kernel(tc, input_seq, W_ih_words, W_ih_scales, b_ih, gh
             nc.scalar.activation(out=zc[u][:], in_=a_z[:], func=ACT.Sigmoid, scale=-1.0)
 
         def on_scalar(u):
-            return u % 2 == 1 and u < N_UNITS - SCALAR_FREE_UNITS
+            return u % 2 == 1 and EARLY_UNITS <= u < N_UNITS - SCALAR_FREE_UNITS
 
         def candidate_sum_on_vector(u):
             bn = b_col[:, GATE_N * BLOCKS + u % BLOCKS : GATE_N * BLOCKS + u % BLOCKS + 1]
@@ -256,25 +263,33 @@ def tile_grucellmodel_pa_kernel(tc, input_seq, W_ih_words, W_ih_scales, b_ih, gh
             engine.tensor_tensor(out=h[:], in0=zc[u][:], in1=n_new[u][:], op=MULT)
             nc.sync.dma_start(out=out[:, c * T_GROUP : (c + 1) * T_GROUP, jb * P : (jb + 1) * P], in_=h[:])
 
-        bt = psum.tile([P, P], BF16, tag="mx", name="bt", bufs=MX_BUFS)
-        nc.tensor.transpose(bt[:], b_rows[:], ident_bf16[:])
-        nc.vector.tensor_copy(out=b_col[:], in_=bt[:, 0 : 3 * BLOCKS])
-        for pair in range(PAIRS):
-            regroup_x(pair)
-        for pair in range(PAIRS):
-            quantise_x(pair)
-        gt_r = psum.tile([P, BLOCKS, P], BF16, tag="mx", name="gt_r", bufs=MX_BUFS)
-        nc.scalar.copy(out=ghT_r[:], in_=transpose_gh(GATE_R, gt_r)[:])
-        matmul_r(0)
-        transpose_gh(GATE_N, ghT_n)
-        nc.scalar.copy(out=ghT_n_sb[:], in_=ghT_n[:])
-        spread_bz()
+        with tc.manual_schedule(engines={mybir.EngineType.PE, mybir.EngineType.DVE, mybir.EngineType.Activation}):
+            for pair in range(PAIRS):
+                regroup_x(pair)
+            for pair in range(PAIRS):
+                quantise_x(pair)
+            bt = psum.tile([P, P], BF16, tag="mx", name="bt", bufs=MX_BUFS)
+            nc.tensor.transpose(bt[:], b_rows[:], ident_bf16[:])
+            nc.vector.tensor_copy(out=b_col[:], in_=bt[:, 0 : 3 * BLOCKS])
+            gt_r = psum.tile([P, BLOCKS, P], BF16, tag="mx", name="gt_r", bufs=MX_BUFS)
+            transpose_gh(GATE_R, gt_r, 0, FIRST_BLOCKS)
+            nc.scalar.copy(out=ghT_r[:, 0:FIRST_BLOCKS, :], in_=gt_r[:, 0:FIRST_BLOCKS, :])
+            matmul_r(0)
+            matmul_r(1)
+            reset_gate(0)
+            reset_gate(1)
+            gt_r = psum.tile([P, BLOCKS, P], BF16, tag="mx", name="gt_r", bufs=MX_BUFS)
+            transpose_gh(GATE_R, gt_r, FIRST_BLOCKS, BLOCKS)
+            nc.vector.tensor_copy(out=ghT_r[:, FIRST_BLOCKS:BLOCKS, :], in_=gt_r[:, FIRST_BLOCKS:BLOCKS, :])
+            transpose_gh(GATE_N, ghT_n)
+            nc.scalar.copy(out=ghT_n_sb[:], in_=ghT_n[:])
+            spread_bz()
 
         def in_range(u):
             return 0 <= u < N_UNITS
 
         for step in range(N_UNITS + OUT_LAG):
-            if in_range(step + 1):
+            if in_range(step + 1) and step + 1 >= FIRST_BLOCKS:
                 matmul_r(step + 1)
             if in_range(step + 1 - Z_LAG):
                 matmul_z(step + 1 - Z_LAG)
@@ -283,7 +298,9 @@ def tile_grucellmodel_pa_kernel(tc, input_seq, W_ih_words, W_ih_scales, b_ih, gh
             if in_range(step - SUM_LAG) and on_scalar(step - SUM_LAG):
                 candidate_bias_on_scalar(step - SUM_LAG)
             if in_range(step):
-                reset_gate(step)
+                if step >= FIRST_BLOCKS:
+                    reset_gate(step)
+                reset_product(step)
             if step == Z_LAG:
                 add_bz_to_gh()
             if in_range(step - Z_LAG):

@@ -31,9 +31,10 @@ SUM_LAG = 2
 TRANSPOSE_LAG = 3
 TANH_LAG = 4
 OUT_LAG = 5
+VECTOR_OUT_LAG = 4
 MX_BUFS = 5
 SCALAR_FREE_UNITS = 6
-VECTOR_OUT_UNITS = 2
+VECTOR_OUT_UNITS = 4
 WARM_UP_MATMULS = 4
 EARLY_UNITS = 6
 FIRST_BLOCKS = 2
@@ -112,17 +113,19 @@ def tile_grucellmodel_pa_kernel(tc, input_seq, W_ih_words, W_ih_scales, b_ih, gh
                 x_words = x_sb[pair][:, tt, :].bitcast(F32)
                 for u in range(2):
                     nc.tensor.transpose(xt[:, tt, u, :], x_words[:, u:WORDS:2], ident_f32[:])
-            grouped[pair] = work.tile([P, 2 * P * 4], BF16, align_bytes=64, name="grouped")
+            c, half = divmod(pair, PAIRS)
+            if half == 0:
+                grouped[c] = work.tile([P, T_GROUP * P * 4], BF16, align_bytes=64, name="grouped")
             copy = nc.vector.tensor_copy if pair == 1 else nc.scalar.copy
             copy(
-                out=grouped[pair][:].bitcast(F32).rearrange("p (t b u) -> p t b u", t=2, u=2),
+                out=grouped[c][:, half * 2 * P * 4 : (half + 1) * 2 * P * 4].bitcast(F32).rearrange("p (t b u) -> p t b u", t=2, u=2),
                 in_=xt[:].rearrange("p t u b -> p t b u"),
             )
 
-        def quantise_x(pair):
-            cols = slice(pair * 2 * P, (pair + 1) * 2 * P)
+        def quantise_x(c, first=0, last=T_GROUP):
+            cols = slice((c * T_GROUP + first) * P, (c * T_GROUP + last) * P)
             nc.vector.quantize_mx(
-                out=x_codes[:, cols].bitcast(FP8X4), scales=x_scales[:, cols], in_=grouped[pair][:]
+                out=x_codes[:, cols].bitcast(FP8X4), scales=x_scales[:, cols], in_=grouped[c][:, first * P * 4 : last * P * 4]
             )
 
         def w_block(gate, jb):
@@ -239,6 +242,9 @@ def tile_grucellmodel_pa_kernel(tc, input_seq, W_ih_words, W_ih_scales, b_ih, gh
             s[u] = work.tile([P, T_GROUP, P], F32, name="s", bufs=3)
             nc.scalar.activation(out=s[u][:], in_=pn[u][:], func=ACT.Identity, bias=bn)
 
+        def vector_out(u):
+            return u >= N_UNITS - VECTOR_OUT_UNITS
+
         def candidate_transpose(u):
             st[u] = psum.tile([P, T_GROUP, P], F32, tag="t", name="st")
             for tt in range(T_GROUP):
@@ -250,24 +256,28 @@ def tile_grucellmodel_pa_kernel(tc, input_seq, W_ih_words, W_ih_scales, b_ih, gh
                         st[u][:, tt, :], lhsT=m[u][:, tt, :], rhs=ident_f32[:], is_transpose=True, start=False, stop=True
                     )
                 else:
-                    nc.tensor.transpose(st[u][:, tt, :], s[u][:, tt, :], ident_f32[:])
+                    source = n_new[u] if vector_out(u) else s[u]
+                    nc.tensor.transpose(st[u][:, tt, :], source[:, tt, :], ident_f32[:])
 
         def candidate_tanh(u):
             n_new[u] = work.tile([P, T_GROUP, P], F32, name="n_new", bufs=3)
-            nc.scalar.activation(out=n_new[u][:], in_=st[u][:], func=ACT.Tanh)
+            source = s[u] if vector_out(u) else st[u]
+            nc.scalar.activation(out=n_new[u][:], in_=source[:], func=ACT.Tanh)
 
         def output(u):
             c, jb = divmod(u, BLOCKS)
             h = work.tile([P, T_GROUP, P], F32, name="h", bufs=4)
-            engine = nc.vector if u >= N_UNITS - VECTOR_OUT_UNITS else nc.gpsimd
-            engine.tensor_tensor(out=h[:], in0=zc[u][:], in1=n_new[u][:], op=MULT)
+            if vector_out(u):
+                nc.vector.tensor_tensor(out=h[:], in0=st[u][:], in1=zc[u][:], op=MULT)
+            else:
+                nc.gpsimd.tensor_tensor(out=h[:], in0=zc[u][:], in1=n_new[u][:], op=MULT)
             nc.sync.dma_start(out=out[:, c * T_GROUP : (c + 1) * T_GROUP, jb * P : (jb + 1) * P], in_=h[:])
 
         with tc.manual_schedule(engines={mybir.EngineType.PE, mybir.EngineType.DVE, mybir.EngineType.Activation}):
             for pair in range(PAIRS):
                 regroup_x(pair)
             for pair in range(PAIRS):
-                quantise_x(pair)
+                quantise_x(0, 2 * pair, 2 * pair + 2)
             bt = psum.tile([P, P], BF16, tag="mx", name="bt", bufs=MX_BUFS)
             nc.tensor.transpose(bt[:], b_rows[:], ident_bf16[:])
             nc.vector.tensor_copy(out=b_col[:], in_=bt[:, 0 : 3 * BLOCKS])
@@ -307,13 +317,17 @@ def tile_grucellmodel_pa_kernel(tc, input_seq, W_ih_words, W_ih_scales, b_ih, gh
                 update_gate(step - Z_LAG)
             if in_range(step - SUM_LAG) and not on_scalar(step - SUM_LAG):
                 candidate_sum_on_vector(step - SUM_LAG)
+                if vector_out(step - SUM_LAG):
+                    candidate_tanh(step - SUM_LAG)
             if in_range(step - TRANSPOSE_LAG):
                 candidate_transpose(step - TRANSPOSE_LAG)
-            if in_range(step - TANH_LAG):
+            if in_range(step - TANH_LAG) and not vector_out(step - TANH_LAG):
                 candidate_tanh(step - TANH_LAG)
+            if in_range(step - VECTOR_OUT_LAG) and vector_out(step - VECTOR_OUT_LAG):
+                output(step - VECTOR_OUT_LAG)
             if PAIRS <= step < N_GROUPS * PAIRS:
                 regroup_x(step)
-            if in_range(step - OUT_LAG):
+            if in_range(step - OUT_LAG) and not vector_out(step - OUT_LAG):
                 output(step - OUT_LAG)
-            if PAIRS <= step - 1 < N_GROUPS * PAIRS:
-                quantise_x(step - 1)
+            if PAIRS <= step - 2 < N_GROUPS * PAIRS and step % PAIRS == 0:
+                quantise_x((step - 2) // PAIRS)

from contextlib import ExitStack

import concourse.mybir as mybir
from concourse.masks import make_identity

F32 = mybir.dt.float32
BF16 = mybir.dt.bfloat16
I32 = mybir.dt.int32
U32 = mybir.dt.uint32
U8 = mybir.dt.uint8
FP8X4 = mybir.dt.float8_e4m3fn_x4
FP4X4 = mybir.dt.float4_e2m1fn_x4
ADD = mybir.AluOpType.add
MULT = mybir.AluOpType.mult
ACT = mybir.ActivationFunctionType

P = 128
T_STEPS = 16
K = 512
H = 1024
BANK = 512
T_GROUP = BANK // P
N_GROUPS = T_STEPS // T_GROUP
PAIRS = T_GROUP // 2
BLOCKS = H // P
N_UNITS = N_GROUPS * BLOCKS
WORDS = K // 2
GATE_R, GATE_Z, GATE_N = 0, 1, 2
Z_LAG = 2
SUM_LAG = 2
TRANSPOSE_LAG = 3
TANH_LAG = 4
OUT_LAG = 5
VECTOR_OUT_LAG = 4
MX_BUFS = 5
SCALAR_FREE_UNITS = 6
VECTOR_OUT_UNITS = 4
WARM_UP_MATMULS = 4
EARLY_UNITS = 6
FIRST_BLOCKS = 2

FLOPS = 2 * T_STEPS * P * K * 3 * H


def tile_grucellmodel_pa_kernel(tc, input_seq, W_ih_words, W_ih_scales, b_ih, gh, out):
    nc = tc.nc
    with ExitStack() as ctx:
        const = ctx.enter_context(tc.tile_pool(name="const", bufs=1))
        work = ctx.enter_context(tc.tile_pool(name="work", bufs=2))
        psum = ctx.enter_context(tc.psum_pool(name="psum", bufs=2))

        zeros = const.tile([P, P], BF16)
        nc.vector.memset(zeros[:], 0.0)
        warm = const.tile([P, 1], F32)
        nc.vector.memset(warm[:], 0.0)
        nc.scalar.activation(out=warm[:], in_=warm[:], func=ACT.Sigmoid)
        ident_f32 = const.tile([P, P], F32)
        make_identity(nc, ident_f32[:])
        ident_bf16 = const.tile([P, P], BF16)
        make_identity(nc, ident_bf16[:])
        for i in range(WARM_UP_MATMULS):
            idle = psum.tile([P, BANK], F32, tag="mx", name="idle", bufs=MX_BUFS)
            nc.tensor.matmul(
                idle[:], lhsT=zeros[:], rhs=zeros[:].unsqueeze(1).to_broadcast([P, T_GROUP, P]), start=True, stop=True
            )
        b_rows = const.tile([P, P], BF16)
        nc.vector.memset(b_rows[:], 0.0)
        w_scales = const.tile([P, 3 * H], U8, align_bytes=64)
        nc.vector.memset(w_scales[:].bitcast(I32), 0)

        x_sb = []
        for pair in range(N_GROUPS * PAIRS):
            x_sb.append(const.tile([P, 2, K], BF16, name="x_sb%d" % pair))
        w_words = const.tile([P, 2 * 3 * H], U8, align_bytes=64)
        gh_sb = const.tile([P, 3 * H], BF16)

        def load_x(pair):
            nc.sync.dma_start(out=x_sb[pair][:], in_=input_seq[2 * pair : 2 * pair + 2].rearrange("t b k -> b t k"))

        def load_w(gate):
            nc.sync.dma_start(
                out=w_words[:, 2 * gate * H : 2 * (gate + 1) * H].bitcast(I32),
                in_=W_ih_words[0, :, 2 * gate * H : 2 * (gate + 1) * H].bitcast(I32),
            )

        def load_gh(gate):
            nc.sync.dma_start(out=gh_sb[:, gate * H : (gate + 1) * H], in_=gh[:, gate * H : (gate + 1) * H])

        for pair in range(PAIRS):
            load_x(pair)
        nc.sync.dma_start(out=b_rows[0 : 3 * BLOCKS, :], in_=b_ih.rearrange("(c p) -> c p", p=P))
        load_w(GATE_R)
        load_gh(GATE_R)
        for q in range(4):
            nc.sync.dma_start(
                out=w_scales[32 * q : 32 * q + 4, :].bitcast(I32),
                in_=W_ih_scales[0, 4 * q : 4 * q + 4, :].bitcast(I32),
            )
        load_gh(GATE_Z)
        load_gh(GATE_N)
        load_w(GATE_Z)
        load_w(GATE_N)
        for pair in range(PAIRS, N_GROUPS * PAIRS):
            load_x(pair)

        x_codes = const.tile([P, T_STEPS * P], U32, align_bytes=64)
        x_scales = const.tile([P, T_STEPS * P], U8, align_bytes=64)
        grouped = {}

        def regroup_x(pair):
            xt = psum.tile([P, 2, 2, P], F32, tag="t", name="xt")
            for tt in range(2):
                x_words = x_sb[pair][:, tt, :].bitcast(F32)
                for u in range(2):
                    nc.tensor.transpose(xt[:, tt, u, :], x_words[:, u:WORDS:2], ident_f32[:])
            c, half = divmod(pair, PAIRS)
            if half == 0:
                grouped[c] = work.tile([P, T_GROUP * P * 4], BF16, align_bytes=64, name="grouped")
            copy = nc.vector.tensor_copy if pair == 1 else nc.scalar.copy
            copy(
                out=grouped[c][:, half * 2 * P * 4 : (half + 1) * 2 * P * 4].bitcast(F32).rearrange("p (t b u) -> p t b u", t=2, u=2),
                in_=xt[:].rearrange("p t u b -> p t b u"),
            )

        def quantise_x(c, first=0, last=T_GROUP):
            cols = slice((c * T_GROUP + first) * P, (c * T_GROUP + last) * P)
            nc.vector.quantize_mx(
                out=x_codes[:, cols].bitcast(FP8X4), scales=x_scales[:, cols], in_=grouped[c][:, first * P * 4 : last * P * 4]
            )

        def w_block(gate, jb):
            first = gate * H + jb * P
            return (w_words[:, 2 * first : 2 * (first + P)].bitcast(FP4X4), w_scales[:, first : first + P])

        def x_block(first, width):
            return (x_codes[:, first : first + width].bitcast(FP8X4), x_scales[:, first : first + width])

        def over_time(block):
            return block.unsqueeze(1).to_broadcast([P, T_GROUP, P])

        def flat(tile3):
            return tile3.rearrange("p t b -> p (t b)")

        b_col = const.tile([P, 3 * BLOCKS], F32)
        ghT_r = const.tile([P, BLOCKS, P], BF16)
        ghT_n = psum.tile([P, BLOCKS, P], BF16, tag="g", name="ghT_n", bufs=1)
        ghT_n_sb = const.tile([P, BLOCKS, P], BF16)
        ghb_z = const.tile([P, H], F32)

        def transpose_gh(gate, gt, first_block=0, last_block=BLOCKS):
            for jb in range(first_block, last_block):
                first = gate * H + jb * P
                nc.tensor.transpose(gt[:, jb, :], gh_sb[:, first : first + P], ident_bf16[:])
            return gt

        bz = {}

        def spread_bz():
            for half in range(H // BANK):
                bz[half] = psum.tile([P, BANK], F32, tag="t", name="bz")
                for i in range(BANK // P):
                    c = GATE_Z * BLOCKS + half * (BANK // P) + i
                    nc.tensor.matmul(
                        bz[half][:, i * P : (i + 1) * P],
                        lhsT=ident_bf16[:, c : c + 1].to_broadcast([P, P]),
                        rhs=b_rows[:],
                        start=True,
                        stop=True,
                    )

        def add_bz_to_gh():
            for half in range(H // BANK):
                nc.vector.tensor_tensor(
                    out=ghb_z[:, half * BANK : (half + 1) * BANK],
                    in0=bz[half][:],
                    in1=gh_sb[:, GATE_Z * H + half * BANK : GATE_Z * H + (half + 1) * BANK],
                    op=ADD,
                )

        pr, pz, pn, st = {}, {}, {}, {}
        r, m, s, zc, n_new = {}, {}, {}, {}, {}

        def matmul_transposed(acc, gate, u):
            c, jb = divmod(u, BLOCKS)
            w, w_scale = w_block(gate, jb)
            x, x_scale = x_block(c * BANK, BANK)
            nc.tensor.matmul_mx(flat(acc[:]), lhsT=w, lhsT_scale=w_scale, rhs=x, rhs_scale=x_scale, start=True, stop=True)

        def matmul_r(u):
            pr[u] = psum.tile([P, T_GROUP, P], F32, tag="mx", name="pr", bufs=MX_BUFS)
            matmul_transposed(pr[u], GATE_R, u)

        def matmul_n(u):
            pn[u] = psum.tile([P, T_GROUP, P], F32, tag="mx", name="pn", bufs=MX_BUFS)
            matmul_transposed(pn[u], GATE_N, u)

        def matmul_z(u):
            c, jb = divmod(u, BLOCKS)
            w, w_scale = w_block(GATE_Z, jb)
            pz[u] = psum.tile([P, T_GROUP, P], F32, tag="mx", name="pz", bufs=MX_BUFS)
            for tt in range(T_GROUP):
                x, x_scale = x_block((c * T_GROUP + tt) * P, P)
                nc.tensor.matmul_mx(pz[u][:, tt, :], lhsT=x, lhsT_scale=x_scale, rhs=w, rhs_scale=w_scale, start=True, stop=True)

        def m_on_gpsimd(u):
            return on_scalar(u) or u < EARLY_UNITS

        def reset_gate(u):
            jb = u % BLOCKS
            a_r = work.tile([P, T_GROUP, P], F32, name="a_r")
            nc.vector.tensor_tensor(out=a_r[:], in0=pr[u][:], in1=over_time(ghT_r[:, jb, :]), op=ADD)
            r[u] = work.tile([P, T_GROUP, P], F32, name="r", bufs=3)
            nc.scalar.activation(out=r[u][:], in_=a_r[:], func=ACT.Sigmoid, bias=b_col[:, jb : jb + 1])

        def reset_product(u):
            jb = u % BLOCKS
            m[u] = work.tile([P, T_GROUP, P], F32, name="m", bufs=5)
            if m_on_gpsimd(u):
                nc.gpsimd.tensor_tensor(out=m[u][:], in0=r[u][:], in1=over_time(ghT_n_sb[:, jb, :]), op=MULT)
            else:
                nc.vector.tensor_tensor(out=m[u][:], in0=r[u][:], in1=over_time(ghT_n[:, jb, :]), op=MULT)

        def update_gate(u):
            jb = u % BLOCKS
            a_z = work.tile([P, T_GROUP, P], F32, name="a_z")
            nc.vector.tensor_tensor(out=a_z[:], in0=pz[u][:], in1=over_time(ghb_z[:, jb * P : (jb + 1) * P]), op=ADD)
            zc[u] = work.tile([P, T_GROUP, P], F32, name="zc", bufs=5)
            nc.scalar.activation(out=zc[u][:], in_=a_z[:], func=ACT.Sigmoid, scale=-1.0)

        def on_scalar(u):
            return u % 2 == 1 and EARLY_UNITS <= u < N_UNITS - SCALAR_FREE_UNITS

        def candidate_sum_on_vector(u):
            bn = b_col[:, GATE_N * BLOCKS + u % BLOCKS : GATE_N * BLOCKS + u % BLOCKS + 1]
            s[u] = work.tile([P, T_GROUP, P], F32, name="s", bufs=3)
            nc.vector.scalar_tensor_tensor(
                out=flat(s[u][:]), in0=flat(pn[u][:]), scalar=bn, in1=flat(m[u][:]), op0=ADD, op1=ADD
            )

        def candidate_bias_on_scalar(u):
            bn = b_col[:, GATE_N * BLOCKS + u % BLOCKS : GATE_N * BLOCKS + u % BLOCKS + 1]
            s[u] = work.tile([P, T_GROUP, P], F32, name="s", bufs=3)
            nc.scalar.activation(out=s[u][:], in_=pn[u][:], func=ACT.Identity, bias=bn)

        def vector_out(u):
            return u >= N_UNITS - VECTOR_OUT_UNITS

        def candidate_transpose(u):
            st[u] = psum.tile([P, T_GROUP, P], F32, tag="t", name="st")
            for tt in range(T_GROUP):
                if on_scalar(u):
                    nc.tensor.matmul(
                        st[u][:, tt, :], lhsT=s[u][:, tt, :], rhs=ident_f32[:], is_transpose=True, start=True, stop=False
                    )
                    nc.tensor.matmul(
                        st[u][:, tt, :], lhsT=m[u][:, tt, :], rhs=ident_f32[:], is_transpose=True, start=False, stop=True
                    )
                else:
                    source = n_new[u] if vector_out(u) else s[u]
                    nc.tensor.transpose(st[u][:, tt, :], source[:, tt, :], ident_f32[:])

        def candidate_tanh(u):
            n_new[u] = work.tile([P, T_GROUP, P], F32, name="n_new", bufs=3)
            source = s[u] if vector_out(u) else st[u]
            nc.scalar.activation(out=n_new[u][:], in_=source[:], func=ACT.Tanh)

        def output(u):
            c, jb = divmod(u, BLOCKS)
            h = work.tile([P, T_GROUP, P], F32, name="h", bufs=4)
            if vector_out(u):
                nc.vector.tensor_tensor(out=h[:], in0=st[u][:], in1=zc[u][:], op=MULT)
            else:
                nc.gpsimd.tensor_tensor(out=h[:], in0=zc[u][:], in1=n_new[u][:], op=MULT)
            nc.sync.dma_start(out=out[:, c * T_GROUP : (c + 1) * T_GROUP, jb * P : (jb + 1) * P], in_=h[:])

        with tc.manual_schedule(engines={mybir.EngineType.PE, mybir.EngineType.DVE, mybir.EngineType.Activation}):
            for pair in range(PAIRS):
                regroup_x(pair)
            for pair in range(PAIRS):
                quantise_x(0, 2 * pair, 2 * pair + 2)
            bt = psum.tile([P, P], BF16, tag="mx", name="bt", bufs=MX_BUFS)
            nc.tensor.transpose(bt[:], b_rows[:], ident_bf16[:])
            nc.vector.tensor_copy(out=b_col[:], in_=bt[:, 0 : 3 * BLOCKS])
            gt_r = psum.tile([P, BLOCKS, P], BF16, tag="mx", name="gt_r", bufs=MX_BUFS)
            transpose_gh(GATE_R, gt_r, 0, FIRST_BLOCKS)
            nc.scalar.copy(out=ghT_r[:, 0:FIRST_BLOCKS, :], in_=gt_r[:, 0:FIRST_BLOCKS, :])
            matmul_r(0)
            matmul_r(1)
            reset_gate(0)
            reset_gate(1)
            gt_r = psum.tile([P, BLOCKS, P], BF16, tag="mx", name="gt_r", bufs=MX_BUFS)
            transpose_gh(GATE_R, gt_r, FIRST_BLOCKS, BLOCKS)
            nc.vector.tensor_copy(out=ghT_r[:, FIRST_BLOCKS:BLOCKS, :], in_=gt_r[:, FIRST_BLOCKS:BLOCKS, :])
            transpose_gh(GATE_N, ghT_n)
            nc.scalar.copy(out=ghT_n_sb[:], in_=ghT_n[:])
            spread_bz()

        def in_range(u):
            return 0 <= u < N_UNITS

        for step in range(N_UNITS + OUT_LAG):
            if in_range(step + 1) and step + 1 >= FIRST_BLOCKS:
                matmul_r(step + 1)
            if in_range(step + 1 - Z_LAG):
                matmul_z(step + 1 - Z_LAG)
            if in_range(step + 1 - SUM_LAG):
                matmul_n(step + 1 - SUM_LAG)
            if in_range(step - SUM_LAG) and on_scalar(step - SUM_LAG):
                candidate_bias_on_scalar(step - SUM_LAG)
            if in_range(step):
                if step >= FIRST_BLOCKS:
                    reset_gate(step)
                reset_product(step)
            if step == Z_LAG:
                add_bz_to_gh()
            if in_range(step - Z_LAG):
                update_gate(step - Z_LAG)
            if in_range(step - SUM_LAG) and not on_scalar(step - SUM_LAG):
                candidate_sum_on_vector(step - SUM_LAG)
                if vector_out(step - SUM_LAG):
                    candidate_tanh(step - SUM_LAG)
            if in_range(step - TRANSPOSE_LAG):
                candidate_transpose(step - TRANSPOSE_LAG)
            if in_range(step - TANH_LAG) and not vector_out(step - TANH_LAG):
                candidate_tanh(step - TANH_LAG)
            if in_range(step - VECTOR_OUT_LAG) and vector_out(step - VECTOR_OUT_LAG):
                output(step - VECTOR_OUT_LAG)
            if PAIRS <= step < N_GROUPS * PAIRS:
                regroup_x(step)
            if in_range(step - OUT_LAG) and not vector_out(step - OUT_LAG):
                output(step - OUT_LAG)
            if PAIRS <= step - 2 < N_GROUPS * PAIRS and step % PAIRS == 0:
                quantise_x((step - 2) // PAIRS)
